import numpy as np
import ml_dtypes


def mxq(x, axis, fmt="e4m3"):
    dtype, down = {"e4m3": (ml_dtypes.float8_e4m3fn, 7), "e5m2": (ml_dtypes.float8_e5m2, 14)}[fmt]
    v = np.moveaxis(np.asarray(x, np.float32).astype(ml_dtypes.bfloat16).astype(np.float64), axis, -1)
    blocks = v.reshape(v.shape[:-1] + (-1, 32))
    amax = np.abs(blocks).max(-1, keepdims=True)
    byte = np.maximum(np.where(amax > 0, np.frexp(amax)[1] - 1 + 127, 0) - down, 1)
    scale = np.exp2(byte - 127.0)
    codes = (blocks / scale).astype(np.float32).astype(dtype).astype(np.float64)
    return np.moveaxis((codes * scale).reshape(v.shape), -1, axis)


WIDE = False


def mx_kscale(k):
    if not WIDE:
        return np.ones(k)
    levels = np.array([10, -10, 5, -5, 0])
    a = np.random.permutation(np.resize(levels, k // 512 * 4)).reshape(k // 512, 4)
    idx = np.arange(k)
    return np.exp2(a[idx // 512, idx % 128 // 32])


BF16 = ml_dtypes.bfloat16


def bf(x):
    return np.asarray(x, np.float32).astype(BF16)


def f64(x):
    return np.asarray(x).astype(np.float64)


B, S, D, H, DH, DFF = 2, 256, 1024, 8, 128, 4096
E = H * DH
THETA = 10000.0
EPS = 1e-5


def rmsnorm(v, g):
    return v * (1.0 / np.sqrt(np.mean(v * v, axis=-1, keepdims=True) + EPS)) * g


def to_heads(t):
    return t.reshape(B, S, H, DH).transpose(0, 2, 1, 3)


def rope(t):
    inv_freq = THETA ** (-(np.arange(0, DH, 2) / DH))
    ang = np.arange(S)[:, None] * inv_freq[None, :]
    cos, sin = np.cos(ang), np.sin(ang)
    t1, t2 = t[..., 0::2], t[..., 1::2]
    r1 = t1 * cos - t2 * sin
    r2 = t1 * sin + t2 * cos
    return np.stack([r1, r2], axis=-1).reshape(t.shape)


def setup_inputs():
    s = mx_kscale(D)
    return {"x": bf(np.random.standard_normal((B, S, D))),
            "wq": bf(np.random.standard_normal((E, D)) / np.sqrt(D) / s[None, :]),
            "wk": bf(np.random.standard_normal((E, D)) / np.sqrt(D) / s[None, :]),
            "ln1_w": bf((1.0 + 0.1 * np.random.standard_normal(D)) * s)}


def reference(x, wq, wk, ln1_w):
    h = rmsnorm(f64(x), f64(ln1_w))
    hq = mxq(h, 2, "e4m3")
    q = to_heads(hq @ mxq(f64(wq), 1, "e4m3").T)
    k = to_heads(hq @ mxq(f64(wk), 1, "e4m3").T)
    return rope(q), rope(k)

@@ -1,0 +1,232 @@
+import math
+
+import concourse.mybir as mybir
+from concourse.masks import make_identity
+
+F32 = mybir.dt.float32
+BF16 = mybir.dt.bfloat16
+I32 = mybir.dt.int32
+U32 = mybir.dt.uint32
+U8 = mybir.dt.uint8
+FP8X4 = mybir.dt.float8_e4m3fn_x4
+ALU = mybir.AluOpType
+ACT = mybir.ActivationFunctionType
+
+P = 128
+B, S, D, H, DH = 2, 256, 1024, 8, 128
+THETA = 10000.0
+EPS = 1e-5
+
+PACK = 4
+K_PASS = P * PACK
+PASSES = D // K_PASS
+TILES_PER_BATCH = S // P
+TOKEN_TILES = B * TILES_PER_BATCH
+CHUNK = 512
+HEADS_PER_CHUNK = CHUNK // DH
+ROW_TILES = CHUNK // P
+CHUNKS_PER_WEIGHT = H * DH // CHUNK
+PAIRS = DH // 2
+WORDS = D // 2
+
+TWO_PI_HI = 6.28125
+TWO_PI_LO = 2.0 * math.pi - TWO_PI_HI
+ROUND_MAGIC = 1.5 * 2.0**23
+
+FLOPS = 2 * B * S * D * 2 * H * DH
+
+
+def build_rotation_table(nc, consts, table):
+    pos_int = consts.tile([P, TILES_PER_BATCH], I32)
+    nc.gpsimd.iota(pos_int[:], pattern=[[1, TILES_PER_BATCH]], base=0, channel_multiplier=TILES_PER_BATCH)
+    pos = consts.tile([P, TILES_PER_BATCH], F32)
+    nc.vector.tensor_copy(out=pos[:], in_=pos_int[:])
+
+    ratio = THETA ** (-2.0 / DH)
+    freq = consts.tile([P, PAIRS], F32)
+    nc.vector.memset(freq[:, 0:1], 1.0)
+    have = 1
+    while have < PAIRS:
+        nc.vector.tensor_scalar(
+            out=freq[:, have : 2 * have], in0=freq[:, 0:have], scalar1=ratio**have, scalar2=None, op0=ALU.mult
+        )
+        have *= 2
+
+    angle = consts.tile([P, TILES_PER_BATCH, PAIRS], F32)
+    for j in range(TILES_PER_BATCH):
+        nc.vector.tensor_scalar(
+            out=angle[:, j, :], in0=freq[:], scalar1=pos[:, j : j + 1], scalar2=None, op0=ALU.mult
+        )
+    angle_flat = angle[:].rearrange("p j i -> p (j i)")
+    n_angles = TILES_PER_BATCH * PAIRS
+
+    phases = (0.0, 0.25)
+    turns = consts.tile([P, 2, n_angles], F32)
+    for f, phase in enumerate(phases):
+        nc.vector.tensor_scalar(
+            out=turns[:, f, :], in0=angle_flat, scalar1=1.0 / (2.0 * math.pi), scalar2=phase,
+            op0=ALU.mult, op1=ALU.add,
+        )
+    whole = consts.tile([P, 2, n_angles], F32)
+    nc.vector.tensor_scalar(
+        out=whole[:], in0=turns[:], scalar1=ROUND_MAGIC, scalar2=ROUND_MAGIC, op0=ALU.add, op1=ALU.subtract
+    )
+    nc.vector.tensor_scalar(
+        out=whole[:, 1, :], in0=whole[:, 1, :], scalar1=phases[1], scalar2=None, op0=ALU.subtract
+    )
+    coarse = consts.tile([P, 2, n_angles], F32)
+    nc.vector.scalar_tensor_tensor(
+        out=coarse[:], in0=whole[:], scalar=-TWO_PI_HI,
+        in1=angle_flat.unsqueeze(1).to_broadcast([P, 2, n_angles]), op0=ALU.mult, op1=ALU.add,
+    )
+    reduced = consts.tile([P, 2, TILES_PER_BATCH, PAIRS], F32)
+    nc.vector.scalar_tensor_tensor(
+        out=reduced[:].rearrange("p f j i -> p f (j i)"), in0=whole[:], scalar=-TWO_PI_LO, in1=coarse[:],
+        op0=ALU.mult, op1=ALU.add,
+    )
+
+    factors = table.rearrange("p j r (i e) -> p j r i e", e=2)
+    for_sin, for_cos = reduced[:, 0], reduced[:, 1]
+    nc.scalar.activation(out=factors[:, :, 0, :, 0], in_=for_cos, func=ACT.Sin)
+    nc.scalar.activation(out=factors[:, :, 0, :, 1], in_=for_sin, func=ACT.Sin, scale=-1.0)
+    nc.scalar.activation(out=factors[:, :, 1, :, 0], in_=for_sin, func=ACT.Sin)
+    nc.scalar.activation(out=factors[:, :, 1, :, 1], in_=for_cos, func=ACT.Sin)
+
+
+def tile_transformerblock_pa_kernel(tc, x, wq, wk, ln1_w, out_0, out_1):
+    nc = tc.nc
+    chunks = [(w, o, c) for w, o in ((wq, out_0), (wk, out_1)) for c in range(CHUNKS_PER_WEIGHT)]
+
+    with tc.tile_pool(name="consts", bufs=1) as consts, tc.tile_pool(
+        name="x_rows", bufs=B
+    ) as x_rows, tc.tile_pool(name="w_rows", bufs=len(chunks) * ROW_TILES) as w_rows, tc.tile_pool(
+        name="per_token_tile", bufs=TOKEN_TILES
+    ) as per_token_tile, tc.tile_pool(name="per_chunk", bufs=len(chunks)) as per_chunk, tc.tile_pool(
+        name="rotating", bufs=4
+    ) as rotating, tc.psum_pool(name="flipped", bufs=4) as flipped, tc.psum_pool(name="sums", bufs=4) as sums:
+        gain_row = consts.tile([P, D], BF16)
+        nc.vector.memset(gain_row[:], 0.0)
+        nc.sync.dma_start(out=gain_row[0:1, :], in_=ln1_w.rearrange("(o d) -> o d", o=1))
+        x_sb = []
+        for b in range(B):
+            x_b = x_rows.tile([P, TILES_PER_BATCH * D], BF16)
+            nc.sync.dma_start(out=x_b[:], in_=x[b].rearrange("(p j) d -> p (j d)", j=TILES_PER_BATCH))
+            x_sb.append(x_b)
+        w_sb = []
+        for w, dst, c in chunks:
+            for r in range(ROW_TILES):
+                w_r = w_rows.tile([P, D], BF16)
+                first = c * CHUNK + r * P
+                nc.sync.dma_start(out=w_r[:], in_=w[first : first + P, :])
+                w_sb.append(w_r)
+
+        ident_bf16 = consts.tile([P, P], BF16)
+        make_identity(nc, ident_bf16[:])
+        ident_f32 = consts.tile([P, P], F32)
+        make_identity(nc, ident_f32[:])
+        ones = consts.tile([P, P], BF16)
+        nc.vector.memset(ones[:], 1.0)
+        minus_half = consts.tile([P, 1], F32)
+        nc.gpsimd.memset(minus_half[:], -0.5)
+        table = consts.tile([P, TILES_PER_BATCH, 2, DH], F32)
+        build_rotation_table(nc, consts, table[:])
+
+        gain = consts.tile([P, D], BF16)
+        for half in range(D // CHUNK):
+            cols = slice(half * CHUNK, (half + 1) * CHUNK)
+            spread = flipped.tile([P, CHUNK], F32, tag="bank")
+            nc.tensor.matmul(out=spread[:], lhsT=ones[:], rhs=gain_row[:, cols], start=True, stop=True)
+            nc.scalar.copy(out=gain[:, cols], in_=spread[:])
+
+        h_codes, h_scales = [], []
+        for tt in range(TOKEN_TILES):
+            b, j = divmod(tt, TILES_PER_BATCH)
+            x_tile = x_sb[b][:, j * D : (j + 1) * D]
+            squares = per_token_tile.tile([P, D], BF16)
+            sum_sq = per_token_tile.tile([P, 1], F32)
+            nc.scalar.activation(out=squares[:], in_=x_tile, func=ACT.Square, accum_out=sum_sq[:])
+            mean_sq = per_token_tile.tile([P, 1], F32)
+            nc.gpsimd.tensor_scalar(
+                out=mean_sq[:], in0=sum_sq[:], scalar1=1.0 / D, scalar2=EPS, op0=ALU.mult, op1=ALU.add
+            )
+            rstd = per_token_tile.tile([P, 1], F32)
+            nc.gpsimd.tensor_tensor(out=rstd[:], in0=mean_sq[:], in1=minus_half[:], op=ALU.pow)
+            h = per_token_tile.tile([P, D], BF16)
+            nc.vector.scalar_tensor_tensor(
+                out=h[:], in0=x_tile, scalar=rstd[:], in1=gain[:], op0=ALU.mult, op1=ALU.mult
+            )
+            h_cols = h[:].rearrange("p (gu q e) -> p gu e q", q=P, e=2)
+            h_t = flipped.tile([P, PASSES * PACK, P], BF16, tag="bank")
+            for gu in range(PASSES * 2):
+                for e in range(2):
+                    nc.tensor.transpose(h_t[:, 2 * gu + e, :], h_cols[:, gu, e, :], ident_bf16[:])
+            h_grouped = per_token_tile.tile([P, PASSES * P * PACK], BF16, align_bytes=64)
+            nc.scalar.copy(
+                out=h_grouped[:].rearrange("p (g m t) -> p g m t", g=PASSES, t=PACK),
+                in_=h_t[:].rearrange("p (g t) m -> p g m t", g=PASSES),
+            )
+            codes = per_token_tile.tile([P, PASSES * P], U32, align_bytes=64)
+            scales = per_token_tile.tile([P, PASSES * P], U8, align_bytes=64)
+            nc.vector.quantize_mx(out=codes[:].bitcast(FP8X4), scales=scales[:], in_=h_grouped[:])
+            h_codes.append(codes)
+            h_scales.append(scales)
+
+        def quantise_chunk(n):
+            w_grouped = per_chunk.tile([P, PASSES * CHUNK * PACK], BF16, align_bytes=64)
+            grouped_words = w_grouped[:].bitcast(F32).rearrange("p (g f u) -> p g f u", g=PASSES, u=2)
+            for r in range(ROW_TILES):
+                words = w_sb[n * ROW_TILES + r][:].bitcast(F32)
+                w_t = flipped.tile([P, WORDS // P, P], F32, tag="bank")
+                for gu in range(WORDS // P):
+                    nc.tensor.transpose(w_t[:, gu, :], words[:, gu * P : (gu + 1) * P], ident_f32[:])
+                nc.scalar.copy(
+                    out=grouped_words[:, :, r * P : (r + 1) * P, :],
+                    in_=w_t[:].rearrange("p (g u) f -> p g f u", g=PASSES),
+                )
+            codes = per_chunk.tile([P, PASSES * CHUNK], U32, align_bytes=64)
+            scales = per_chunk.tile([P, PASSES * CHUNK], U8, align_bytes=64)
+            nc.vector.quantize_mx(out=codes[:].bitcast(FP8X4), scales=scales[:], in_=w_grouped[:])
+            return codes, scales
+
+        def project_and_rotate(n, w_codes, w_scales):
+            w, dst, c = chunks[n]
+            heads = slice(c * HEADS_PER_CHUNK, (c + 1) * HEADS_PER_CHUNK)
+            for b in range(B):
+                rotated = rotating.tile([P, HEADS_PER_CHUNK, TILES_PER_BATCH, DH], F32)
+                for j in range(TILES_PER_BATCH):
+                    tt = b * TILES_PER_BATCH + j
+                    acc = sums.tile([P, CHUNK], F32)
+                    for g in range(PASSES):
+                        nc.tensor.matmul_mx(
+                            out=acc[:],
+                            lhsT=h_codes[tt][:, g * P : (g + 1) * P].bitcast(FP8X4),
+                            lhsT_scale=h_scales[tt][:, g * P : (g + 1) * P],
+                            rhs=w_codes[:, g * CHUNK : (g + 1) * CHUNK].bitcast(FP8X4),
+                            rhs_scale=w_scales[:, g * CHUNK : (g + 1) * CHUNK],
+                            start=(g == 0),
+                            stop=(g == PASSES - 1),
+                        )
+                    shape = [P, 2, HEADS_PER_CHUNK, DH]
+                    products = rotating.tile(shape, F32)
+                    nc.vector.tensor_tensor(
+                        out=products[:],
+                        in0=acc[:].rearrange("p (h d) -> p h d", d=DH).unsqueeze(1).to_broadcast(shape),
+                        in1=table[:, j].unsqueeze(2).to_broadcast(shape),
+                        op=ALU.mult,
+                    )
+                    terms = products[:].rearrange("p r h (i e) -> p h i r e", e=2)
+                    nc.gpsimd.tensor_tensor(
+                        out=rotated[:, :, j, :].rearrange("p h (i r) -> p h i r", r=2),
+                        in0=terms[:, :, :, :, 0],
+                        in1=terms[:, :, :, :, 1],
+                        op=ALU.add,
+                    )
+                nc.sync.dma_start(
+                    out=dst[b, heads].rearrange("h (p j) d -> p h j d", j=TILES_PER_BATCH), in_=rotated[:]
+                )
+
+        ready = quantise_chunk(0)
+        for n in range(len(chunks)):
+            following = quantise_chunk(n + 1) if n + 1 < len(chunks) else None
+            project_and_rotate(n, ready[0], ready[1])
+            ready = following

@@ -5,7 +5,6 @@ from concourse.masks import make_identity
 
 F32 = mybir.dt.float32
 BF16 = mybir.dt.bfloat16
-I32 = mybir.dt.int32
 U32 = mybir.dt.uint32
 U8 = mybir.dt.uint8
 FP8X4 = mybir.dt.float8_e4m3fn_x4
@@ -29,68 +28,10 @@ CHUNKS_PER_WEIGHT = H * DH // CHUNK
 PAIRS = DH // 2
 WORDS = D // 2
 
-TWO_PI_HI = 6.28125
-TWO_PI_LO = 2.0 * math.pi - TWO_PI_HI
 ROUND_MAGIC = 1.5 * 2.0**23
+PHASES = (0.5, 0.25, 0.0)
 
 FLOPS = 2 * B * S * D * 2 * H * DH
-
-
-def build_rotation_table(nc, consts, table):
-    pos_int = consts.tile([P, TILES_PER_BATCH], I32)
-    nc.gpsimd.iota(pos_int[:], pattern=[[1, TILES_PER_BATCH]], base=0, channel_multiplier=TILES_PER_BATCH)
-    pos = consts.tile([P, TILES_PER_BATCH], F32)
-    nc.vector.tensor_copy(out=pos[:], in_=pos_int[:])
-
-    ratio = THETA ** (-2.0 / DH)
-    freq = consts.tile([P, PAIRS], F32)
-    nc.vector.memset(freq[:, 0:1], 1.0)
-    have = 1
-    while have < PAIRS:
-        nc.vector.tensor_scalar(
-            out=freq[:, have : 2 * have], in0=freq[:, 0:have], scalar1=ratio**have, scalar2=None, op0=ALU.mult
-        )
-        have *= 2
-
-    angle = consts.tile([P, TILES_PER_BATCH, PAIRS], F32)
-    for j in range(TILES_PER_BATCH):
-        nc.vector.tensor_scalar(
-            out=angle[:, j, :], in0=freq[:], scalar1=pos[:, j : j + 1], scalar2=None, op0=ALU.mult
-        )
-    angle_flat = angle[:].rearrange("p j i -> p (j i)")
-    n_angles = TILES_PER_BATCH * PAIRS
-
-    phases = (0.0, 0.25)
-    turns = consts.tile([P, 2, n_angles], F32)
-    for f, phase in enumerate(phases):
-        nc.vector.tensor_scalar(
-            out=turns[:, f, :], in0=angle_flat, scalar1=1.0 / (2.0 * math.pi), scalar2=phase,
-            op0=ALU.mult, op1=ALU.add,
-        )
-    whole = consts.tile([P, 2, n_angles], F32)
-    nc.vector.tensor_scalar(
-        out=whole[:], in0=turns[:], scalar1=ROUND_MAGIC, scalar2=ROUND_MAGIC, op0=ALU.add, op1=ALU.subtract
-    )
-    nc.vector.tensor_scalar(
-        out=whole[:, 1, :], in0=whole[:, 1, :], scalar1=phases[1], scalar2=None, op0=ALU.subtract
-    )
-    coarse = consts.tile([P, 2, n_angles], F32)
-    nc.vector.scalar_tensor_tensor(
-        out=coarse[:], in0=whole[:], scalar=-TWO_PI_HI,
-        in1=angle_flat.unsqueeze(1).to_broadcast([P, 2, n_angles]), op0=ALU.mult, op1=ALU.add,
-    )
-    reduced = consts.tile([P, 2, TILES_PER_BATCH, PAIRS], F32)
-    nc.vector.scalar_tensor_tensor(
-        out=reduced[:].rearrange("p f j i -> p f (j i)"), in0=whole[:], scalar=-TWO_PI_LO, in1=coarse[:],
-        op0=ALU.mult, op1=ALU.add,
-    )
-
-    factors = table.rearrange("p j r (i e) -> p j r i e", e=2)
-    for_sin, for_cos = reduced[:, 0], reduced[:, 1]
-    nc.scalar.activation(out=factors[:, :, 0, :, 0], in_=for_cos, func=ACT.Sin)
-    nc.scalar.activation(out=factors[:, :, 0, :, 1], in_=for_sin, func=ACT.Sin, scale=-1.0)
-    nc.scalar.activation(out=factors[:, :, 1, :, 0], in_=for_sin, func=ACT.Sin)
-    nc.scalar.activation(out=factors[:, :, 1, :, 1], in_=for_cos, func=ACT.Sin)
 
 
 def tile_transformerblock_pa_kernel(tc, x, wq, wk, ln1_w, out_0, out_1):
@@ -98,135 +39,257 @@ def tile_transformerblock_pa_kernel(tc, x, wq, wk, ln1_w, out_0, out_1):
     chunks = [(w, o, c) for w, o in ((wq, out_0), (wk, out_1)) for c in range(CHUNKS_PER_WEIGHT)]
 
     with tc.tile_pool(name="consts", bufs=1) as consts, tc.tile_pool(
-        name="x_rows", bufs=B
-    ) as x_rows, tc.tile_pool(name="w_rows", bufs=len(chunks) * ROW_TILES) as w_rows, tc.tile_pool(
-        name="per_token_tile", bufs=TOKEN_TILES
-    ) as per_token_tile, tc.tile_pool(name="per_chunk", bufs=len(chunks)) as per_chunk, tc.tile_pool(
-        name="rotating", bufs=4
-    ) as rotating, tc.psum_pool(name="flipped", bufs=4) as flipped, tc.psum_pool(name="sums", bufs=4) as sums:
-        gain_row = consts.tile([P, D], BF16)
-        nc.vector.memset(gain_row[:], 0.0)
-        nc.sync.dma_start(out=gain_row[0:1, :], in_=ln1_w.rearrange("(o d) -> o d", o=1))
-        x_sb = []
-        for b in range(B):
-            x_b = x_rows.tile([P, TILES_PER_BATCH * D], BF16)
-            nc.sync.dma_start(out=x_b[:], in_=x[b].rearrange("(p j) d -> p (j d)", j=TILES_PER_BATCH))
-            x_sb.append(x_b)
-        w_sb = []
-        for w, dst, c in chunks:
+        name="w_rows", bufs=len(chunks) * ROW_TILES
+    ) as w_rows, tc.tile_pool(name="per_token_tile", bufs=TOKEN_TILES) as per_token_tile, tc.tile_pool(
+        name="per_chunk", bufs=len(chunks)
+    ) as per_chunk, tc.tile_pool(name="rotating", bufs=6) as rotating, tc.psum_pool(
+        name="flipped", bufs=4
+    ) as flipped, tc.psum_pool(name="spread", bufs=1) as spread, tc.psum_pool(
+        name="sums", bufs=3
+    ) as sums, tc.manual_schedule():
+        x_sb = {}
+        w_sb = {}
+
+        def load_x(tt):
+            b, j = divmod(tt, TILES_PER_BATCH)
+            x_t = per_token_tile.tile([P, D], BF16)
+            nc.sync.dma_start(out=x_t[:], in_=x[b].rearrange("(p j) d -> p j d", j=TILES_PER_BATCH)[:, j, :])
+            x_sb[tt] = x_t
+
+        def load_w(n):
+            w, dst, c = chunks[n]
             for r in range(ROW_TILES):
                 w_r = w_rows.tile([P, D], BF16)
                 first = c * CHUNK + r * P
                 nc.sync.dma_start(out=w_r[:], in_=w[first : first + P, :])
-                w_sb.append(w_r)
+                w_sb[n, r] = w_r
 
-        ident_bf16 = consts.tile([P, P], BF16)
-        make_identity(nc, ident_bf16[:])
-        ident_f32 = consts.tile([P, P], F32)
-        make_identity(nc, ident_f32[:])
+        minus_half = consts.tile([P, 2], F32)
+        nc.gpsimd.memset(minus_half[:], -0.5)
+        pos = consts.tile([P, TILES_PER_BATCH], F32)
+        nc.gpsimd.iota(
+            pos[:], pattern=[[1, TILES_PER_BATCH]], base=0, channel_multiplier=TILES_PER_BATCH,
+            allow_small_or_imprecise_dtypes=True,
+        )
+        ident = consts.tile([P, P], F32)
+        make_identity(nc, ident[:])
+
+        gain_row = consts.tile([P, D], BF16)
+        nc.vector.memset(gain_row[:].bitcast(F32), 0.0)
+        load_x(0)
+        nc.sync.dma_start(out=gain_row[0:1, :], in_=ln1_w.rearrange("(o d) -> o d", o=1))
+        load_x(1)
+        load_w(0)
+        load_x(2)
+        load_x(3)
+        for n in range(1, len(chunks)):
+            load_w(n)
+
+        warm = consts.tile([P, 2], F32)
+        nc.scalar.activation(out=warm[:], in_=minus_half[:], func=ACT.Sin)
+
         ones = consts.tile([P, P], BF16)
         nc.vector.memset(ones[:], 1.0)
-        minus_half = consts.tile([P, 1], F32)
-        nc.gpsimd.memset(minus_half[:], -0.5)
-        table = consts.tile([P, TILES_PER_BATCH, 2, DH], F32)
-        build_rotation_table(nc, consts, table[:])
 
-        gain = consts.tile([P, D], BF16)
+        ratio = THETA ** (-2.0 / DH)
+        freq = consts.tile([P, PAIRS], F32)
+        nc.vector.memset(freq[:, 0:1], 1.0)
+        have = 1
+        while have < PAIRS:
+            nc.vector.tensor_scalar(
+                out=freq[:, have : 2 * have], in0=freq[:, 0:have], scalar1=ratio**have, scalar2=None, op0=ALU.mult
+            )
+            have *= 2
+        turns = consts.tile([P, len(PHASES), TILES_PER_BATCH, PAIRS], F32)
+        for j in range(TILES_PER_BATCH):
+            nc.vector.tensor_scalar(
+                out=turns[:, 2, j, :], in0=freq[:], scalar1=pos[:, j : j + 1], scalar2=1.0 / (2.0 * math.pi),
+                op0=ALU.mult, op1=ALU.mult,
+            )
+
+        gain = spread.tile([P, D], BF16)
         for half in range(D // CHUNK):
             cols = slice(half * CHUNK, (half + 1) * CHUNK)
-            spread = flipped.tile([P, CHUNK], F32, tag="bank")
-            nc.tensor.matmul(out=spread[:], lhsT=ones[:], rhs=gain_row[:, cols], start=True, stop=True)
-            nc.scalar.copy(out=gain[:, cols], in_=spread[:])
+            nc.tensor.matmul(out=gain[:, cols], lhsT=ones[:], rhs=gain_row[:, cols], start=True, stop=True)
 
-        h_codes, h_scales = [], []
-        for tt in range(TOKEN_TILES):
-            b, j = divmod(tt, TILES_PER_BATCH)
-            x_tile = x_sb[b][:, j * D : (j + 1) * D]
+        def square_on_vector(tt, mean_col):
             squares = per_token_tile.tile([P, D], BF16)
-            sum_sq = per_token_tile.tile([P, 1], F32)
-            nc.scalar.activation(out=squares[:], in_=x_tile, func=ACT.Square, accum_out=sum_sq[:])
-            mean_sq = per_token_tile.tile([P, 1], F32)
-            nc.gpsimd.tensor_scalar(
-                out=mean_sq[:], in0=sum_sq[:], scalar1=1.0 / D, scalar2=EPS, op0=ALU.mult, op1=ALU.add
+            nc.vector.scalar_tensor_tensor(
+                out=squares[:], in0=x_sb[tt][:], scalar=1.0 / D, in1=x_sb[tt][:], op0=ALU.mult, op1=ALU.mult,
+                accum_out=mean_col,
             )
-            rstd = per_token_tile.tile([P, 1], F32)
-            nc.gpsimd.tensor_tensor(out=rstd[:], in0=mean_sq[:], in1=minus_half[:], op=ALU.pow)
+
+        def square_on_scalar(tt, mean_col):
+            squares = per_token_tile.tile([P, D], BF16)
+            nc.scalar.activation(
+                out=squares[:], in_=x_sb[tt][:], func=ACT.Square, scale=D**-0.5, accum_out=mean_col
+            )
+
+        def inverse_root(mean_sq):
+            shifted = per_token_tile.tile([P, TILES_PER_BATCH], F32)
+            nc.gpsimd.tensor_scalar(
+                out=shifted[:], in0=mean_sq[:], scalar1=1.0, scalar2=EPS, op0=ALU.mult, op1=ALU.add
+            )
+            rstd = per_token_tile.tile([P, TILES_PER_BATCH], F32)
+            nc.gpsimd.tensor_tensor(out=rstd[:], in0=shifted[:], in1=minus_half[:], op=ALU.pow)
+            return rstd
+
+        def normalise(tt, rstd):
+            j = tt % TILES_PER_BATCH
             h = per_token_tile.tile([P, D], BF16)
             nc.vector.scalar_tensor_tensor(
-                out=h[:], in0=x_tile, scalar=rstd[:], in1=gain[:], op0=ALU.mult, op1=ALU.mult
+                out=h[:], in0=x_sb[tt][:], scalar=rstd[:, j : j + 1], in1=gain[:], op0=ALU.mult, op1=ALU.mult
             )
-            h_cols = h[:].rearrange("p (gu q e) -> p gu e q", q=P, e=2)
-            h_t = flipped.tile([P, PASSES * PACK, P], BF16, tag="bank")
-            for gu in range(PASSES * 2):
-                for e in range(2):
-                    nc.tensor.transpose(h_t[:, 2 * gu + e, :], h_cols[:, gu, e, :], ident_bf16[:])
+            return h
+
+        def flip(rows):
+            words = rows[:].bitcast(F32)
+            bank = flipped.tile([P, WORDS // P, P], F32)
+            for gu in range(WORDS // P):
+                nc.tensor.transpose(bank[:, gu, :], words[:, gu * P : (gu + 1) * P], ident[:])
+            return bank
+
+        h_codes, h_scales = {}, {}
+
+        def group_h(tt, bank):
             h_grouped = per_token_tile.tile([P, PASSES * P * PACK], BF16, align_bytes=64)
             nc.scalar.copy(
-                out=h_grouped[:].rearrange("p (g m t) -> p g m t", g=PASSES, t=PACK),
-                in_=h_t[:].rearrange("p (g t) m -> p g m t", g=PASSES),
+                out=h_grouped[:].bitcast(F32).rearrange("p (g m u) -> p g m u", g=PASSES, u=2),
+                in_=bank[:].rearrange("p (g u) m -> p g m u", g=PASSES),
             )
-            codes = per_token_tile.tile([P, PASSES * P], U32, align_bytes=64)
-            scales = per_token_tile.tile([P, PASSES * P], U8, align_bytes=64)
-            nc.vector.quantize_mx(out=codes[:].bitcast(FP8X4), scales=scales[:], in_=h_grouped[:])
-            h_codes.append(codes)
-            h_scales.append(scales)
+            return h_grouped
 
-        def quantise_chunk(n):
-            w_grouped = per_chunk.tile([P, PASSES * CHUNK * PACK], BF16, align_bytes=64)
-            grouped_words = w_grouped[:].bitcast(F32).rearrange("p (g f u) -> p g f u", g=PASSES, u=2)
+        def quantise_h(tt, h_grouped):
+            hc = per_token_tile.tile([P, PASSES * P], U32, align_bytes=64)
+            hs = per_token_tile.tile([P, PASSES * P], U8, align_bytes=64)
+            nc.vector.quantize_mx(out=hc[:].bitcast(FP8X4), scales=hs[:], in_=h_grouped[:])
+            h_codes[tt], h_scales[tt] = hc, hs
+
+        w_grouped = {}
+        w_codes, w_scales = {}, {}
+
+        def flip_and_group_w(n):
+            w_grouped[n] = per_chunk.tile([P, PASSES * CHUNK * PACK], BF16, align_bytes=64, name="w_group")
+            words = w_grouped[n][:].bitcast(F32).rearrange("p (g f u) -> p g f u", g=PASSES, u=2)
             for r in range(ROW_TILES):
-                words = w_sb[n * ROW_TILES + r][:].bitcast(F32)
-                w_t = flipped.tile([P, WORDS // P, P], F32, tag="bank")
-                for gu in range(WORDS // P):
-                    nc.tensor.transpose(w_t[:, gu, :], words[:, gu * P : (gu + 1) * P], ident_f32[:])
+                bank = flip(w_sb[n, r])
                 nc.scalar.copy(
-                    out=grouped_words[:, :, r * P : (r + 1) * P, :],
-                    in_=w_t[:].rearrange("p (g u) f -> p g f u", g=PASSES),
+                    out=words[:, :, r * P : (r + 1) * P, :],
+                    in_=bank[:].rearrange("p (g u) f -> p g f u", g=PASSES),
                 )
+
+        def quantise_w(n):
             codes = per_chunk.tile([P, PASSES * CHUNK], U32, align_bytes=64)
             scales = per_chunk.tile([P, PASSES * CHUNK], U8, align_bytes=64)
-            nc.vector.quantize_mx(out=codes[:].bitcast(FP8X4), scales=scales[:], in_=w_grouped[:])
-            return codes, scales
+            nc.vector.quantize_mx(out=codes[:].bitcast(FP8X4), scales=scales[:], in_=w_grouped[n][:])
+            w_codes[n], w_scales[n] = codes, scales
 
-        def project_and_rotate(n, w_codes, w_scales):
+        table = consts.tile([P, TILES_PER_BATCH, 2, DH], F32)
+
+        def multiply(n, tt):
+            acc = sums.tile([P, CHUNK], F32)
+            for g in range(PASSES):
+                nc.tensor.matmul_mx(
+                    out=acc[:],
+                    lhsT=h_codes[tt][:, g * P : (g + 1) * P].bitcast(FP8X4),
+                    lhsT_scale=h_scales[tt][:, g * P : (g + 1) * P],
+                    rhs=w_codes[n][:, g * CHUNK : (g + 1) * CHUNK].bitcast(FP8X4),
+                    rhs_scale=w_scales[n][:, g * CHUNK : (g + 1) * CHUNK],
+                    start=(g == 0),
+                    stop=(g == PASSES - 1),
+                )
+            return acc
+
+        rotated = {}
+
+        def rotate(n, tt, acc, adder):
+            b, j = divmod(tt, TILES_PER_BATCH)
+            shape = [P, 2, HEADS_PER_CHUNK, PAIRS, 2]
+            products = rotating.tile(shape, F32)
+            nc.vector.tensor_tensor(
+                out=products[:],
+                in0=acc[:].rearrange("p (h i e) -> p e h i", i=PAIRS, e=2).unsqueeze(4).to_broadcast(shape),
+                in1=table[:, j].rearrange("p e (i r) -> p e i r", r=2).unsqueeze(2).to_broadcast(shape),
+                op=ALU.mult,
+            )
+            if j == 0:
+                rotated[n, b] = rotating.tile([P, HEADS_PER_CHUNK, TILES_PER_BATCH, DH], F32, name="turned")
+            adder.tensor_tensor(
+                out=rotated[n, b][:, :, j, :],
+                in0=products[:, 0].rearrange("p h i r -> p h (i r)"),
+                in1=products[:, 1].rearrange("p h i r -> p h (i r)"),
+                op=ALU.add,
+            )
+
+        def store(n, b, js=slice(0, TILES_PER_BATCH)):
             w, dst, c = chunks[n]
             heads = slice(c * HEADS_PER_CHUNK, (c + 1) * HEADS_PER_CHUNK)
-            for b in range(B):
-                rotated = rotating.tile([P, HEADS_PER_CHUNK, TILES_PER_BATCH, DH], F32)
-                for j in range(TILES_PER_BATCH):
-                    tt = b * TILES_PER_BATCH + j
-                    acc = sums.tile([P, CHUNK], F32)
-                    for g in range(PASSES):
-                        nc.tensor.matmul_mx(
-                            out=acc[:],
-                            lhsT=h_codes[tt][:, g * P : (g + 1) * P].bitcast(FP8X4),
-                            lhsT_scale=h_scales[tt][:, g * P : (g + 1) * P],
-                            rhs=w_codes[:, g * CHUNK : (g + 1) * CHUNK].bitcast(FP8X4),
-                            rhs_scale=w_scales[:, g * CHUNK : (g + 1) * CHUNK],
-                            start=(g == 0),
-                            stop=(g == PASSES - 1),
-                        )
-                    shape = [P, 2, HEADS_PER_CHUNK, DH]
-                    products = rotating.tile(shape, F32)
-                    nc.vector.tensor_tensor(
-                        out=products[:],
-                        in0=acc[:].rearrange("p (h d) -> p h d", d=DH).unsqueeze(1).to_broadcast(shape),
-                        in1=table[:, j].unsqueeze(2).to_broadcast(shape),
-                        op=ALU.mult,
-                    )
-                    terms = products[:].rearrange("p r h (i e) -> p h i r e", e=2)
-                    nc.gpsimd.tensor_tensor(
-                        out=rotated[:, :, j, :].rearrange("p h (i r) -> p h i r", r=2),
-                        in0=terms[:, :, :, :, 0],
-                        in1=terms[:, :, :, :, 1],
-                        op=ALU.add,
-                    )
-                nc.sync.dma_start(
-                    out=dst[b, heads].rearrange("h (p j) d -> p h j d", j=TILES_PER_BATCH), in_=rotated[:]
-                )
+            out_view = dst[b, heads].rearrange("h (p j) d -> p h j d", j=TILES_PER_BATCH)
+            nc.sync.dma_start(out=out_view[:, :, js, :], in_=rotated[n, b][:, :, js, :])
 
-        ready = quantise_chunk(0)
-        for n in range(len(chunks)):
-            following = quantise_chunk(n + 1) if n + 1 < len(chunks) else None
-            project_and_rotate(n, ready[0], ready[1])
-            ready = following
+        mean_first = per_token_tile.tile([P, TILES_PER_BATCH], F32, name="mean_sq")
+        square_on_vector(0, mean_first[:, 0:1])
+        square_on_scalar(1, mean_first[:, 1:2])
+        rstd_first = inverse_root(mean_first)
+
+        for f in range(2):
+            nc.vector.tensor_scalar(
+                out=turns[:, f], in0=turns[:, 2], scalar1=PHASES[f], scalar2=None, op0=ALU.add
+            )
+        whole = consts.tile([P, len(PHASES), TILES_PER_BATCH, PAIRS], F32)
+        nc.vector.tensor_scalar(
+            out=whole[:], in0=turns[:], scalar1=ROUND_MAGIC, scalar2=ROUND_MAGIC, op0=ALU.add, op1=ALU.subtract
+        )
+        part = consts.tile([P, len(PHASES), TILES_PER_BATCH, PAIRS], F32)
+        nc.vector.tensor_tensor(out=part[:], in0=turns[:], in1=whole[:], op=ALU.subtract)
+
+        flip_and_group_w(0)
+        h0 = normalise(0, rstd_first)
+        h1 = normalise(1, rstd_first)
+        for e in range(2):
+            nc.scalar.activation(
+                out=table[:, :, e].rearrange("p j (i r) -> p j i r", r=2),
+                in_=part[:, 1 - e : 3 - e].rearrange("p r j i -> p j i r"),
+                func=ACT.Sin, scale=2.0 * math.pi,
+            )
+        g0 = group_h(0, flip(h0))
+        g1 = group_h(1, flip(h1))
+        quantise_w(0)
+        quantise_h(0, g0)
+        quantise_h(1, g1)
+
+        mean_second = per_token_tile.tile([P, TILES_PER_BATCH], F32, name="mean_sq")
+        square_on_scalar(2, mean_second[:, 0:1])
+        square_on_scalar(3, mean_second[:, 1:2])
+        rstd_second = inverse_root(mean_second)
+
+        rotate(0, 0, multiply(0, 0), nc.gpsimd)
+        rotate(0, 1, multiply(0, 1), nc.gpsimd)
+        store(0, 0)
+        h2 = normalise(2, rstd_second)
+        h3 = normalise(3, rstd_second)
+        flip_and_group_w(1)
+        g2 = group_h(2, flip(h2))
+        g3 = group_h(3, flip(h3))
+        quantise_w(1)
+        quantise_h(2, g2)
+        quantise_h(3, g3)
+        rotate(0, 2, multiply(0, 2), nc.gpsimd)
+        rotate(0, 3, multiply(0, 3), nc.gpsimd)
+        store(0, 1)
+        flip_and_group_w(2)
+
+        for n in range(1, len(chunks)):
+            if n + 2 < len(chunks):
+                flip_and_group_w(n + 2)
+            last = n + 1 == len(chunks)
+            for tt in range(TOKEN_TILES):
+                b, j = divmod(tt, TILES_PER_BATCH)
+                adder = nc.vector if last and tt + 1 == TOKEN_TILES else nc.gpsimd
+                rotate(n, tt, multiply(n, tt), adder)
+                if last and b + 1 == B:
+                    store(n, b, slice(j, j + 1))
+                elif j + 1 == TILES_PER_BATCH:
+                    store(n, b)
+                if tt == 1 and not last:
+                    quantise_w(n + 1)

@@ -20,33 +20,34 @@ PACK = 4
 K_PASS = P * PACK
 PASSES = D // K_PASS
 TILES_PER_BATCH = S // P
-TOKEN_TILES = B * TILES_PER_BATCH
 CHUNK = 512
-HEADS_PER_CHUNK = CHUNK // DH
+HEADS = CHUNK // DH
 ROW_TILES = CHUNK // P
 CHUNKS_PER_WEIGHT = H * DH // CHUNK
+CHUNKS = 2 * CHUNKS_PER_WEIGHT
+TOKEN_TILES = B * TILES_PER_BATCH
 PAIRS = DH // 2
 WORDS = D // 2
 
 ROUND_MAGIC = 1.5 * 2.0**23
-PHASES = (0.5, 0.25, 0.0)
+COS, SIN = range(2)
+QUARTER = 0.25
+TWO_PI = 2.0 * math.pi
 
 FLOPS = 2 * B * S * D * 2 * H * DH
 
 
 def tile_transformerblock_pa_kernel(tc, x, wq, wk, ln1_w, out_0, out_1):
     nc = tc.nc
-    chunks = [(w, o, c) for w, o in ((wq, out_0), (wk, out_1)) for c in range(CHUNKS_PER_WEIGHT)]
-
     with tc.tile_pool(name="consts", bufs=1) as consts, tc.tile_pool(
-        name="w_rows", bufs=len(chunks) * ROW_TILES
+        name="w_rows", bufs=CHUNKS * ROW_TILES
     ) as w_rows, tc.tile_pool(name="per_token_tile", bufs=TOKEN_TILES) as per_token_tile, tc.tile_pool(
-        name="per_chunk", bufs=len(chunks)
-    ) as per_chunk, tc.tile_pool(name="rotating", bufs=6) as rotating, tc.psum_pool(
-        name="flipped", bufs=4
-    ) as flipped, tc.psum_pool(name="spread", bufs=1) as spread, tc.psum_pool(
+        name="per_chunk", bufs=CHUNKS
+    ) as per_chunk, tc.tile_pool(
+        name="rotating", bufs=6
+    ) as rotating, tc.psum_pool(name="flipped", bufs=3) as flipped, tc.psum_pool(
         name="sums", bufs=3
-    ) as sums, tc.manual_schedule():
+    ) as sums, tc.psum_pool(name="back", bufs=2) as back, tc.manual_schedule():
         x_sb = {}
         w_sb = {}
 
@@ -57,14 +58,16 @@ def tile_transformerblock_pa_kernel(tc, x, wq, wk, ln1_w, out_0, out_1):
             x_sb[tt] = x_t
 
         def load_w(n):
-            w, dst, c = chunks[n]
+            matrix, c = divmod(n, CHUNKS_PER_WEIGHT)
             for r in range(ROW_TILES):
                 w_r = w_rows.tile([P, D], BF16)
                 first = c * CHUNK + r * P
-                nc.sync.dma_start(out=w_r[:], in_=w[first : first + P, :])
+                nc.sync.dma_start(out=w_r[:], in_=(wq, wk)[matrix][first : first + P, :])
                 w_sb[n, r] = w_r
 
-        minus_half = consts.tile([P, 2], F32)
+        gain_row = consts.tile([P, D], BF16)
+        nc.gpsimd.memset(gain_row[:].bitcast(F32), 0.0)
+        minus_half = consts.tile([P, 1], F32)
         nc.gpsimd.memset(minus_half[:], -0.5)
         pos = consts.tile([P, TILES_PER_BATCH], F32)
         nc.gpsimd.iota(
@@ -73,19 +76,21 @@ def tile_transformerblock_pa_kernel(tc, x, wq, wk, ln1_w, out_0, out_1):
         )
         ident = consts.tile([P, P], F32)
         make_identity(nc, ident[:])
+        swap = consts.tile([P, P], F32)
+        for r in range(2):
+            nc.gpsimd.tensor_copy(
+                out=swap[:].rearrange("p (i r) -> p i r", r=2)[:, :, r],
+                in_=ident[:].rearrange("p (i r) -> p i r", r=2)[:, :, 1 - r],
+            )
 
-        gain_row = consts.tile([P, D], BF16)
-        nc.vector.memset(gain_row[:].bitcast(F32), 0.0)
         load_x(0)
         nc.sync.dma_start(out=gain_row[0:1, :], in_=ln1_w.rearrange("(o d) -> o d", o=1))
-        load_x(1)
-        load_w(0)
-        load_x(2)
-        load_x(3)
-        for n in range(1, len(chunks)):
+        for tt in range(1, TOKEN_TILES):
+            load_x(tt)
+        for n in range(CHUNKS):
             load_w(n)
 
-        warm = consts.tile([P, 2], F32)
+        warm = consts.tile([P, 1], F32)
         nc.scalar.activation(out=warm[:], in_=minus_half[:], func=ACT.Sin)
 
         ones = consts.tile([P, P], BF16)
@@ -100,196 +105,266 @@ def tile_transformerblock_pa_kernel(tc, x, wq, wk, ln1_w, out_0, out_1):
                 out=freq[:, have : 2 * have], in0=freq[:, 0:have], scalar1=ratio**have, scalar2=None, op0=ALU.mult
             )
             have *= 2
-        turns = consts.tile([P, len(PHASES), TILES_PER_BATCH, PAIRS], F32)
+        turns = consts.tile([P, 2, TILES_PER_BATCH, PAIRS], F32)
         for j in range(TILES_PER_BATCH):
             nc.vector.tensor_scalar(
-                out=turns[:, 2, j, :], in0=freq[:], scalar1=pos[:, j : j + 1], scalar2=1.0 / (2.0 * math.pi),
+                out=turns[:, SIN, j, :], in0=freq[:], scalar1=pos[:, j : j + 1], scalar2=1.0 / TWO_PI,
                 op0=ALU.mult, op1=ALU.mult,
             )
+        whole = consts.tile([P, 2, TILES_PER_BATCH, PAIRS], F32)
+        part = consts.tile([P, 2, TILES_PER_BATCH, PAIRS], F32)
 
-        gain = spread.tile([P, D], BF16)
-        for half in range(D // CHUNK):
-            cols = slice(half * CHUNK, (half + 1) * CHUNK)
+        def reduce_angles():
+            nc.vector.tensor_scalar(
+                out=turns[:, COS], in0=turns[:, SIN], scalar1=QUARTER, scalar2=None, op0=ALU.add
+            )
+            nc.vector.tensor_scalar(
+                out=whole[:], in0=turns[:], scalar1=ROUND_MAGIC, scalar2=ROUND_MAGIC, op0=ALU.add, op1=ALU.subtract
+            )
+            nc.vector.tensor_tensor(out=part[:], in0=turns[:], in1=whole[:], op=ALU.subtract)
+
+        gain = back.tile([P, D], BF16, tag="bank")
+        for half in range(2):
+            cols = slice(half * D // 2, (half + 1) * D // 2)
             nc.tensor.matmul(out=gain[:, cols], lhsT=ones[:], rhs=gain_row[:, cols], start=True, stop=True)
 
-        def square_on_vector(tt, mean_col):
+        def mean_square(tt):
+            half = D // 2
             squares = per_token_tile.tile([P, D], BF16)
+            by_vector = per_token_tile.tile([P, 1], F32)
             nc.vector.scalar_tensor_tensor(
-                out=squares[:], in0=x_sb[tt][:], scalar=1.0 / D, in1=x_sb[tt][:], op0=ALU.mult, op1=ALU.mult,
-                accum_out=mean_col,
+                out=squares[:, :half], in0=x_sb[tt][:, :half], scalar=1.0 / D, in1=x_sb[tt][:, :half],
+                op0=ALU.mult, op1=ALU.mult, accum_out=by_vector[:],
             )
-
-        def square_on_scalar(tt, mean_col):
-            squares = per_token_tile.tile([P, D], BF16)
+            by_scalar = per_token_tile.tile([P, 1], F32)
             nc.scalar.activation(
-                out=squares[:], in_=x_sb[tt][:], func=ACT.Square, scale=D**-0.5, accum_out=mean_col
+                out=squares[:, half:], in_=x_sb[tt][:, half:], func=ACT.Square, scale=D**-0.5, accum_out=by_scalar[:]
             )
+            return by_vector, by_scalar
 
-        def inverse_root(mean_sq):
-            shifted = per_token_tile.tile([P, TILES_PER_BATCH], F32)
-            nc.gpsimd.tensor_scalar(
-                out=shifted[:], in0=mean_sq[:], scalar1=1.0, scalar2=EPS, op0=ALU.mult, op1=ALU.add
+        def mean_square_on_scalar(tt):
+            squares = per_token_tile.tile([P, D], BF16)
+            by_scalar = per_token_tile.tile([P, 1], F32)
+            nc.scalar.activation(
+                out=squares[:], in_=x_sb[tt][:], func=ACT.Square, scale=D**-0.5, accum_out=by_scalar[:]
             )
-            rstd = per_token_tile.tile([P, TILES_PER_BATCH], F32)
+            return (by_scalar,)
+
+        def inverse_root(sums_of_squares):
+            shifted = per_token_tile.tile([P, 1], F32)
+            if len(sums_of_squares) == 2:
+                nc.gpsimd.tensor_scalar(
+                    out=shifted[:], in0=sums_of_squares[0][:], scalar1=sums_of_squares[1][:], scalar2=EPS, op0=ALU.add, op1=ALU.add
+                )
+            else:
+                nc.gpsimd.tensor_scalar(
+                    out=shifted[:], in0=sums_of_squares[0][:], scalar1=1.0, scalar2=EPS, op0=ALU.mult, op1=ALU.add
+                )
+            rstd = per_token_tile.tile([P, 1], F32)
             nc.gpsimd.tensor_tensor(out=rstd[:], in0=shifted[:], in1=minus_half[:], op=ALU.pow)
             return rstd
 
         def normalise(tt, rstd):
-            j = tt % TILES_PER_BATCH
             h = per_token_tile.tile([P, D], BF16)
             nc.vector.scalar_tensor_tensor(
-                out=h[:], in0=x_sb[tt][:], scalar=rstd[:, j : j + 1], in1=gain[:], op0=ALU.mult, op1=ALU.mult
+                out=h[:], in0=x_sb[tt][:], scalar=rstd[:], in1=gain[:], op0=ALU.mult, op1=ALU.mult
             )
             return h
 
-        def flip(rows):
+        h_grouped, h_codes, h_scales = {}, {}, {}
+        w_grouped, w_codes, w_scales = {}, {}, {}
+
+        def flip_and_group(rows, grouped, slot):
             words = rows[:].bitcast(F32)
-            bank = flipped.tile([P, WORDS // P, P], F32)
+            bank = flipped.tile([P, WORDS // P, P], F32, tag="bank")
             for gu in range(WORDS // P):
                 nc.tensor.transpose(bank[:, gu, :], words[:, gu * P : (gu + 1) * P], ident[:])
-            return bank
-
-        h_codes, h_scales = {}, {}
-
-        def group_h(tt, bank):
-            h_grouped = per_token_tile.tile([P, PASSES * P * PACK], BF16, align_bytes=64)
+            view = grouped[:].bitcast(F32).rearrange("p (g c u) -> p g c u", g=PASSES, u=2)
             nc.scalar.copy(
-                out=h_grouped[:].bitcast(F32).rearrange("p (g m u) -> p g m u", g=PASSES, u=2),
-                in_=bank[:].rearrange("p (g u) m -> p g m u", g=PASSES),
+                out=view[:, :, slot * P : (slot + 1) * P, :], in_=bank[:].rearrange("p (g u) c -> p g c u", g=PASSES)
             )
-            return h_grouped
 
-        def quantise_h(tt, h_grouped):
-            hc = per_token_tile.tile([P, PASSES * P], U32, align_bytes=64)
-            hs = per_token_tile.tile([P, PASSES * P], U8, align_bytes=64)
-            nc.vector.quantize_mx(out=hc[:].bitcast(FP8X4), scales=hs[:], in_=h_grouped[:])
-            h_codes[tt], h_scales[tt] = hc, hs
-
-        w_grouped = {}
-        w_codes, w_scales = {}, {}
-
-        def flip_and_group_w(n):
-            w_grouped[n] = per_chunk.tile([P, PASSES * CHUNK * PACK], BF16, align_bytes=64, name="w_group")
-            words = w_grouped[n][:].bitcast(F32).rearrange("p (g f u) -> p g f u", g=PASSES, u=2)
-            for r in range(ROW_TILES):
-                bank = flip(w_sb[n, r])
-                nc.scalar.copy(
-                    out=words[:, :, r * P : (r + 1) * P, :],
-                    in_=bank[:].rearrange("p (g u) f -> p g f u", g=PASSES),
-                )
+        def group_w(n, rows=range(ROW_TILES)):
+            if n not in w_grouped:
+                w_grouped[n] = per_chunk.tile([P, PASSES * CHUNK * PACK], BF16, align_bytes=64, name="w_group")
+            for r in rows:
+                flip_and_group(w_sb[n, r], w_grouped[n], r)
 
         def quantise_w(n):
-            codes = per_chunk.tile([P, PASSES * CHUNK], U32, align_bytes=64)
-            scales = per_chunk.tile([P, PASSES * CHUNK], U8, align_bytes=64)
-            nc.vector.quantize_mx(out=codes[:].bitcast(FP8X4), scales=scales[:], in_=w_grouped[n][:])
-            w_codes[n], w_scales[n] = codes, scales
+            wc = per_chunk.tile([P, PASSES * CHUNK], U32, align_bytes=64)
+            ws = per_chunk.tile([P, PASSES * CHUNK], U8, align_bytes=64)
+            nc.vector.quantize_mx(out=wc[:].bitcast(FP8X4), scales=ws[:], in_=w_grouped[n][:])
+            w_codes[n], w_scales[n] = wc, ws
 
-        table = consts.tile([P, TILES_PER_BATCH, 2, DH], F32)
+        def group_h(tt, h):
+            h_grouped[tt] = per_token_tile.tile([P, PASSES * P * PACK], BF16, align_bytes=64, name="h_group")
+            flip_and_group(h, h_grouped[tt], 0)
+
+        def quantise_h(tt):
+            hc = per_token_tile.tile([P, PASSES * P], U32, align_bytes=64)
+            hs = per_token_tile.tile([P, PASSES * P], U8, align_bytes=64)
+            nc.vector.quantize_mx(out=hc[:].bitcast(FP8X4), scales=hs[:], in_=h_grouped[tt][:])
+            h_codes[tt], h_scales[tt] = hc, hs
+
+        pairwise = consts.tile([P, TILES_PER_BATCH, 2, DH], F32)
+        straight = consts.tile([P, TILES_PER_BATCH, 2, DH], F32)
+        across = consts.tile([P, 2, S], F32)
+
+        by_pair = "p j (i r) -> p j i r"
+
+        def sines(out, kind, scale=TWO_PI):
+            nc.scalar.activation(out=out, in_=kind, func=ACT.Sin, scale=scale)
+
+        def fill_pairwise():
+            first, second = (pairwise[:, :, e].rearrange(by_pair, r=2) for e in range(2))
+            sines(first, part[:].rearrange("p r j i -> p j i r"))
+            sines(second[:, :, :, 0], part[:, SIN], scale=-TWO_PI)
+            sines(second[:, :, :, 1], part[:, COS])
+
+        def fill_straight():
+            same, other = (straight[:, :, which].rearrange(by_pair, r=2) for which in range(2))
+            shape = [P, TILES_PER_BATCH, PAIRS, 2]
+            sines(same, part[:, COS].unsqueeze(3).to_broadcast(shape))
+            sines(other[:, :, :, 0], part[:, SIN])
+            sines(other[:, :, :, 1], part[:, SIN], scale=-TWO_PI)
+
+        def turn_tables():
+            bank = flipped.tile([P, 2, TILES_PER_BATCH, P], F32, tag="bank")
+            for which in range(2):
+                for j in range(TILES_PER_BATCH):
+                    nc.tensor.transpose(bank[:, which, j, :], straight[:, j, which, :], ident[:])
+            nc.scalar.copy(out=across[:], in_=bank[:].rearrange("p w j t -> p w (j t)"))
+
+        def in_feature_form(n, tt):
+            return tt == 1 and n > 0
+
+        sums_of, products_of, turned_of = {}, {}, {}
 
         def multiply(n, tt):
             acc = sums.tile([P, CHUNK], F32)
-            for g in range(PASSES):
-                nc.tensor.matmul_mx(
-                    out=acc[:],
-                    lhsT=h_codes[tt][:, g * P : (g + 1) * P].bitcast(FP8X4),
-                    lhsT_scale=h_scales[tt][:, g * P : (g + 1) * P],
-                    rhs=w_codes[n][:, g * CHUNK : (g + 1) * CHUNK].bitcast(FP8X4),
-                    rhs_scale=w_scales[n][:, g * CHUNK : (g + 1) * CHUNK],
-                    start=(g == 0),
-                    stop=(g == PASSES - 1),
+            if in_feature_form(n, tt):
+                for head in range(HEADS):
+                    for g in range(PASSES):
+                        stationary = slice(g * CHUNK + head * P, g * CHUNK + (head + 1) * P)
+                        moving = slice(g * P, (g + 1) * P)
+                        nc.tensor.matmul_mx(
+                            out=acc[:, head * P : (head + 1) * P],
+                            lhsT=w_codes[n][:, stationary].bitcast(FP8X4),
+                            lhsT_scale=w_scales[n][:, stationary],
+                            rhs=h_codes[tt][:, moving].bitcast(FP8X4),
+                            rhs_scale=h_scales[tt][:, moving],
+                            start=(g == 0),
+                            stop=(g == PASSES - 1),
+                        )
+            else:
+                for g in range(PASSES):
+                    stationary = slice(g * P, (g + 1) * P)
+                    moving = slice(g * CHUNK, (g + 1) * CHUNK)
+                    nc.tensor.matmul_mx(
+                        out=acc[:],
+                        lhsT=h_codes[tt][:, stationary].bitcast(FP8X4),
+                        lhsT_scale=h_scales[tt][:, stationary],
+                        rhs=w_codes[n][:, moving].bitcast(FP8X4),
+                        rhs_scale=w_scales[n][:, moving],
+                        start=(g == 0),
+                        stop=(g == PASSES - 1),
+                    )
+            sums_of[n, tt] = acc
+
+        def form_products(n, tt):
+            acc = sums_of.pop((n, tt))
+            j = tt % TILES_PER_BATCH
+            if in_feature_form(n, tt):
+                shape = [P, 2, HEADS, P]
+                products = rotating.tile(shape, F32)
+                nc.vector.tensor_tensor(
+                    out=products[:],
+                    in0=acc[:].rearrange("p (h t) -> p h t", t=P).unsqueeze(1).to_broadcast(shape),
+                    in1=across[:, :, j * P : (j + 1) * P].unsqueeze(2).to_broadcast(shape),
+                    op=ALU.mult,
                 )
-            return acc
+            else:
+                shape = [P, 2, HEADS, PAIRS, 2]
+                products = rotating.tile(shape, F32)
+                nc.vector.tensor_tensor(
+                    out=products[:],
+                    in0=acc[:].rearrange("p (h i e) -> p e h i", i=PAIRS, e=2).unsqueeze(4).to_broadcast(shape),
+                    in1=pairwise[:, j].rearrange("p e (i r) -> p e i r", r=2).unsqueeze(2).to_broadcast(shape),
+                    op=ALU.mult,
+                )
+            products_of[n, tt] = products
 
-        rotated = {}
-
-        def rotate(n, tt, acc, adder):
+        def add_products(n, tt, adder=nc.gpsimd):
+            products = products_of.pop((n, tt))
             b, j = divmod(tt, TILES_PER_BATCH)
-            shape = [P, 2, HEADS_PER_CHUNK, PAIRS, 2]
-            products = rotating.tile(shape, F32)
-            nc.vector.tensor_tensor(
-                out=products[:],
-                in0=acc[:].rearrange("p (h i e) -> p e h i", i=PAIRS, e=2).unsqueeze(4).to_broadcast(shape),
-                in1=table[:, j].rearrange("p e (i r) -> p e i r", r=2).unsqueeze(2).to_broadcast(shape),
-                op=ALU.mult,
-            )
             if j == 0:
-                rotated[n, b] = rotating.tile([P, HEADS_PER_CHUNK, TILES_PER_BATCH, DH], F32, name="turned")
-            adder.tensor_tensor(
-                out=rotated[n, b][:, :, j, :],
-                in0=products[:, 0].rearrange("p h i r -> p h (i r)"),
-                in1=products[:, 1].rearrange("p h i r -> p h (i r)"),
-                op=ALU.add,
-            )
+                turned_of[n, b] = rotating.tile([P, HEADS, TILES_PER_BATCH, DH], F32, name="turned")
+            turned = turned_of[n, b]
+            if in_feature_form(n, tt):
+                bank = back.tile([P, HEADS, DH], F32, tag="bank")
+                for head in range(HEADS):
+                    for which, order in enumerate((ident, swap)):
+                        nc.tensor.matmul(
+                            out=bank[:, head, :], lhsT=products[:, which, head, :], rhs=order[:],
+                            start=(which == 0), stop=(which == 1), is_transpose=True,
+                        )
+                nc.scalar.copy(out=turned[:, :, j, :], in_=bank[:])
+            else:
+                adder.tensor_tensor(
+                    out=turned[:, :, j, :],
+                    in0=products[:, 0].rearrange("p h i r -> p h (i r)"),
+                    in1=products[:, 1].rearrange("p h i r -> p h (i r)"),
+                    op=ALU.add,
+                )
+            matrix, c = divmod(n, CHUNKS_PER_WEIGHT)
+            view = (out_0, out_1)[matrix][b, c * HEADS : (c + 1) * HEADS].rearrange("h (p j) d -> p h j d", j=TILES_PER_BATCH)
+            if n + 1 == CHUNKS and b + 1 == B:
+                nc.sync.dma_start(out=view[:, :, j, :], in_=turned[:, :, j, :])
+            elif j + 1 == TILES_PER_BATCH:
+                nc.sync.dma_start(out=view, in_=turned[:])
 
-        def store(n, b, js=slice(0, TILES_PER_BATCH)):
-            w, dst, c = chunks[n]
-            heads = slice(c * HEADS_PER_CHUNK, (c + 1) * HEADS_PER_CHUNK)
-            out_view = dst[b, heads].rearrange("h (p j) d -> p h j d", j=TILES_PER_BATCH)
-            nc.sync.dma_start(out=out_view[:, :, js, :], in_=rotated[n, b][:, :, js, :])
-
-        mean_first = per_token_tile.tile([P, TILES_PER_BATCH], F32, name="mean_sq")
-        square_on_vector(0, mean_first[:, 0:1])
-        square_on_scalar(1, mean_first[:, 1:2])
-        rstd_first = inverse_root(mean_first)
-
-        for f in range(2):
-            nc.vector.tensor_scalar(
-                out=turns[:, f], in0=turns[:, 2], scalar1=PHASES[f], scalar2=None, op0=ALU.add
-            )
-        whole = consts.tile([P, len(PHASES), TILES_PER_BATCH, PAIRS], F32)
-        nc.vector.tensor_scalar(
-            out=whole[:], in0=turns[:], scalar1=ROUND_MAGIC, scalar2=ROUND_MAGIC, op0=ALU.add, op1=ALU.subtract
-        )
-        part = consts.tile([P, len(PHASES), TILES_PER_BATCH, PAIRS], F32)
-        nc.vector.tensor_tensor(out=part[:], in0=turns[:], in1=whole[:], op=ALU.subtract)
-
-        flip_and_group_w(0)
-        h0 = normalise(0, rstd_first)
-        h1 = normalise(1, rstd_first)
-        for e in range(2):
-            nc.scalar.activation(
-                out=table[:, :, e].rearrange("p j (i r) -> p j i r", r=2),
-                in_=part[:, 1 - e : 3 - e].rearrange("p r j i -> p j i r"),
-                func=ACT.Sin, scale=2.0 * math.pi,
-            )
-        g0 = group_h(0, flip(h0))
-        g1 = group_h(1, flip(h1))
+        squares_0 = mean_square(0)
+        squares_1 = mean_square(1)
+        reduce_angles()
+        rstd_0 = inverse_root(squares_0)
+        rstd_1 = inverse_root(squares_1)
+        rstd_2 = inverse_root(mean_square_on_scalar(2))
+        rstd_3 = inverse_root(mean_square_on_scalar(3))
+        h0 = normalise(0, rstd_0)
+        h1 = normalise(1, rstd_1)
+        h2 = normalise(2, rstd_2)
+        h3 = normalise(3, rstd_3)
+        group_w(0, (0, 1))
+        group_h(0, h0)
+        group_w(0, (2,))
+        group_h(1, h1)
+        group_w(0, (3,))
+        quantise_h(0)
+        group_h(2, h2)
         quantise_w(0)
-        quantise_h(0, g0)
-        quantise_h(1, g1)
-
-        mean_second = per_token_tile.tile([P, TILES_PER_BATCH], F32, name="mean_sq")
-        square_on_scalar(2, mean_second[:, 0:1])
-        square_on_scalar(3, mean_second[:, 1:2])
-        rstd_second = inverse_root(mean_second)
-
-        rotate(0, 0, multiply(0, 0), nc.gpsimd)
-        rotate(0, 1, multiply(0, 1), nc.gpsimd)
-        store(0, 0)
-        h2 = normalise(2, rstd_second)
-        h3 = normalise(3, rstd_second)
-        flip_and_group_w(1)
-        g2 = group_h(2, flip(h2))
-        g3 = group_h(3, flip(h3))
-        quantise_w(1)
-        quantise_h(2, g2)
-        quantise_h(3, g3)
-        rotate(0, 2, multiply(0, 2), nc.gpsimd)
-        rotate(0, 3, multiply(0, 3), nc.gpsimd)
-        store(0, 1)
-        flip_and_group_w(2)
-
-        for n in range(1, len(chunks)):
-            if n + 2 < len(chunks):
-                flip_and_group_w(n + 2)
-            last = n + 1 == len(chunks)
-            for tt in range(TOKEN_TILES):
-                b, j = divmod(tt, TILES_PER_BATCH)
-                adder = nc.vector if last and tt + 1 == TOKEN_TILES else nc.gpsimd
-                rotate(n, tt, multiply(n, tt), adder)
-                if last and b + 1 == B:
-                    store(n, b, slice(j, j + 1))
-                elif j + 1 == TILES_PER_BATCH:
-                    store(n, b)
-                if tt == 1 and not last:
-                    quantise_w(n + 1)
+        fill_pairwise()
+        group_h(3, h3)
+        quantise_h(1)
+        group_w(1, (0,))
+        multiply(0, 0)
+        quantise_h(2)
+        multiply(0, 1)
+        quantise_h(3)
+        group_w(1, (1, 2, 3))
+        order = [(n, tt) for n in range(CHUNKS) for tt in range(TOKEN_TILES)]
+        for k, (n, tt) in enumerate(order):
+            form_products(n, tt)
+            vector_adds = (n, tt) in ((0, 2), (CHUNKS - 1, TOKEN_TILES - 1))
+            if vector_adds:
+                add_products(n, tt, nc.vector)
+            if tt == (2 if n == 0 else 1) and n + 1 < CHUNKS:
+                quantise_w(n + 1)
+            if k + 2 < len(order):
+                multiply(*order[k + 2])
+            if not vector_adds:
+                add_products(n, tt)
+            if k == 2:
+                fill_straight()
+                turn_tables()
+            if n + 2 < CHUNKS:
+                group_w(n + 2, (tt,))

@@ -340,11 +340,11 @@ def tile_transformerblock_pa_kernel(tc, x, wq, wk, ln1_w, out_0, out_1):
         group_h(1, h1)
         group_w(0, (3,))
         quantise_h(0)
+        quantise_h(1)
         group_h(2, h2)
         quantise_w(0)
-        fill_pairwise()
         group_h(3, h3)
-        quantise_h(1)
+        fill_pairwise()
         group_w(1, (0,))
         multiply(0, 0)
         quantise_h(2)
@@ -354,7 +354,7 @@ def tile_transformerblock_pa_kernel(tc, x, wq, wk, ln1_w, out_0, out_1):
         order = [(n, tt) for n in range(CHUNKS) for tt in range(TOKEN_TILES)]
         for k, (n, tt) in enumerate(order):
             form_products(n, tt)
-            vector_adds = (n, tt) in ((0, 2), (CHUNKS - 1, TOKEN_TILES - 1))
+            vector_adds = (n, tt) == order[-1]
             if vector_adds:
                 add_products(n, tt, nc.vector)
             if tt == (2 if n == 0 else 1) and n + 1 < CHUNKS:

@@ -236,7 +236,7 @@ def tile_transformerblock_pa_kernel(tc, x, wq, wk, ln1_w, out_0, out_1):
             nc.scalar.copy(out=across[:], in_=bank[:].rearrange("p w j t -> p w (j t)"))
 
         def in_feature_form(n, tt):
-            return tt == 1 and n > 0
+            return tt < 2 and 0 < n < CHUNKS - 1 or (n, tt) == (CHUNKS - 1, 2)
 
         sums_of, products_of, turned_of = {}, {}, {}
 
@@ -351,6 +351,7 @@ def tile_transformerblock_pa_kernel(tc, x, wq, wk, ln1_w, out_0, out_1):
         multiply(0, 1)
         quantise_h(3)
         group_w(1, (1, 2, 3))
+        fill_straight()
         order = [(n, tt) for n in range(CHUNKS) for tt in range(TOKEN_TILES)]
         for k, (n, tt) in enumerate(order):
             form_products(n, tt)
@@ -363,8 +364,7 @@ def tile_transformerblock_pa_kernel(tc, x, wq, wk, ln1_w, out_0, out_1):
                 multiply(*order[k + 2])
             if not vector_adds:
                 add_products(n, tt)
-            if k == 2:
-                fill_straight()
+            if k == 1:
                 turn_tables()
             if n + 2 < CHUNKS:
                 group_w(n + 2, (tt,))

@@ -193,7 +193,14 @@ def tile_transformerblock_pa_kernel(tc, x, wq, wk, ln1_w, out_0, out_1):
         def quantise_w(n):
             wc = per_chunk.tile([P, PASSES * CHUNK], U32, align_bytes=64)
             ws = per_chunk.tile([P, PASSES * CHUNK], U8, align_bytes=64)
-            nc.vector.quantize_mx(out=wc[:].bitcast(FP8X4), scales=ws[:], in_=w_grouped[n][:])
+            parts = PASSES if n == 0 else 1
+            words = PASSES * CHUNK // parts
+            for part_of in range(parts):
+                nc.vector.quantize_mx(
+                    out=wc[:, part_of * words : (part_of + 1) * words].bitcast(FP8X4),
+                    scales=ws[:, part_of * words : (part_of + 1) * words],
+                    in_=w_grouped[n][:, part_of * words * PACK : (part_of + 1) * words * PACK],
+                )
             w_codes[n], w_scales[n] = wc, ws
 
         def group_h(tt, h):

import math

import concourse.mybir as mybir
from concourse.masks import make_identity

F32 = mybir.dt.float32
BF16 = mybir.dt.bfloat16
U32 = mybir.dt.uint32
U8 = mybir.dt.uint8
FP8X4 = mybir.dt.float8_e4m3fn_x4
ALU = mybir.AluOpType
ACT = mybir.ActivationFunctionType

P = 128
B, S, D, H, DH = 2, 256, 1024, 8, 128
THETA = 10000.0
EPS = 1e-5

PACK = 4
K_PASS = P * PACK
PASSES = D // K_PASS
TILES_PER_BATCH = S // P
CHUNK = 512
HEADS = CHUNK // DH
ROW_TILES = CHUNK // P
CHUNKS_PER_WEIGHT = H * DH // CHUNK
CHUNKS = 2 * CHUNKS_PER_WEIGHT
TOKEN_TILES = B * TILES_PER_BATCH
PAIRS = DH // 2
WORDS = D // 2

ROUND_MAGIC = 1.5 * 2.0**23
COS, SIN = range(2)
QUARTER = 0.25
TWO_PI = 2.0 * math.pi

FLOPS = 2 * B * S * D * 2 * H * DH


def tile_transformerblock_pa_kernel(tc, x, wq, wk, ln1_w, out_0, out_1):
    nc = tc.nc
    with tc.tile_pool(name="consts", bufs=1) as consts, tc.tile_pool(
        name="w_rows", bufs=CHUNKS * ROW_TILES
    ) as w_rows, tc.tile_pool(name="per_token_tile", bufs=TOKEN_TILES) as per_token_tile, tc.tile_pool(
        name="per_chunk", bufs=CHUNKS
    ) as per_chunk, tc.tile_pool(
        name="rotating", bufs=6
    ) as rotating, tc.psum_pool(name="flipped", bufs=3) as flipped, tc.psum_pool(
        name="sums", bufs=3
    ) as sums, tc.psum_pool(name="back", bufs=2) as back, tc.manual_schedule():
        x_sb = {}
        w_sb = {}

        def load_x(tt):
            b, j = divmod(tt, TILES_PER_BATCH)
            x_t = per_token_tile.tile([P, D], BF16)
            nc.sync.dma_start(out=x_t[:], in_=x[b].rearrange("(p j) d -> p j d", j=TILES_PER_BATCH)[:, j, :])
            x_sb[tt] = x_t

        def load_w(n):
            matrix, c = divmod(n, CHUNKS_PER_WEIGHT)
            for r in range(ROW_TILES):
                w_r = w_rows.tile([P, D], BF16)
                first = c * CHUNK + r * P
                nc.sync.dma_start(out=w_r[:], in_=(wq, wk)[matrix][first : first + P, :])
                w_sb[n, r] = w_r

        gain_row = consts.tile([P, D], BF16)
        nc.gpsimd.memset(gain_row[:].bitcast(F32), 0.0)
        minus_half = consts.tile([P, 1], F32)
        nc.gpsimd.memset(minus_half[:], -0.5)
        pos = consts.tile([P, TILES_PER_BATCH], F32)
        nc.gpsimd.iota(
            pos[:], pattern=[[1, TILES_PER_BATCH]], base=0, channel_multiplier=TILES_PER_BATCH,
            allow_small_or_imprecise_dtypes=True,
        )
        ident = consts.tile([P, P], F32)
        make_identity(nc, ident[:])
        swap = consts.tile([P, P], F32)
        for r in range(2):
            nc.gpsimd.tensor_copy(
                out=swap[:].rearrange("p (i r) -> p i r", r=2)[:, :, r],
                in_=ident[:].rearrange("p (i r) -> p i r", r=2)[:, :, 1 - r],
            )

        load_x(0)
        nc.sync.dma_start(out=gain_row[0:1, :], in_=ln1_w.rearrange("(o d) -> o d", o=1))
        for tt in range(1, TOKEN_TILES):
            load_x(tt)
        for n in range(CHUNKS):
            load_w(n)

        warm = consts.tile([P, 1], F32)
        nc.scalar.activation(out=warm[:], in_=minus_half[:], func=ACT.Sin)

        ones = consts.tile([P, P], BF16)
        nc.vector.memset(ones[:], 1.0)

        ratio = THETA ** (-2.0 / DH)
        freq = consts.tile([P, PAIRS], F32)
        nc.vector.memset(freq[:, 0:1], 1.0)
        have = 1
        while have < PAIRS:
            nc.vector.tensor_scalar(
                out=freq[:, have : 2 * have], in0=freq[:, 0:have], scalar1=ratio**have, scalar2=None, op0=ALU.mult
            )
            have *= 2
        turns = consts.tile([P, 2, TILES_PER_BATCH, PAIRS], F32)
        for j in range(TILES_PER_BATCH):
            nc.vector.tensor_scalar(
                out=turns[:, SIN, j, :], in0=freq[:], scalar1=pos[:, j : j + 1], scalar2=1.0 / TWO_PI,
                op0=ALU.mult, op1=ALU.mult,
            )
        whole = consts.tile([P, 2, TILES_PER_BATCH, PAIRS], F32)
        part = consts.tile([P, 2, TILES_PER_BATCH, PAIRS], F32)

        def reduce_angles():
            nc.vector.tensor_scalar(
                out=turns[:, COS], in0=turns[:, SIN], scalar1=QUARTER, scalar2=None, op0=ALU.add
            )
            nc.vector.tensor_scalar(
                out=whole[:], in0=turns[:], scalar1=ROUND_MAGIC, scalar2=ROUND_MAGIC, op0=ALU.add, op1=ALU.subtract
            )
            nc.vector.tensor_tensor(out=part[:], in0=turns[:], in1=whole[:], op=ALU.subtract)

        gain = back.tile([P, D], BF16, tag="bank")
        for half in range(2):
            cols = slice(half * D // 2, (half + 1) * D // 2)
            nc.tensor.matmul(out=gain[:, cols], lhsT=ones[:], rhs=gain_row[:, cols], start=True, stop=True)

        def mean_square(tt):
            half = D // 2
            squares = per_token_tile.tile([P, D], BF16)
            by_vector = per_token_tile.tile([P, 1], F32)
            nc.vector.scalar_tensor_tensor(
                out=squares[:, :half], in0=x_sb[tt][:, :half], scalar=1.0 / D, in1=x_sb[tt][:, :half],
                op0=ALU.mult, op1=ALU.mult, accum_out=by_vector[:],
            )
            by_scalar = per_token_tile.tile([P, 1], F32)
            nc.scalar.activation(
                out=squares[:, half:], in_=x_sb[tt][:, half:], func=ACT.Square, scale=D**-0.5, accum_out=by_scalar[:]
            )
            return by_vector, by_scalar

        def mean_square_on_scalar(tt):
            squares = per_token_tile.tile([P, D], BF16)
            by_scalar = per_token_tile.tile([P, 1], F32)
            nc.scalar.activation(
                out=squares[:], in_=x_sb[tt][:], func=ACT.Square, scale=D**-0.5, accum_out=by_scalar[:]
            )
            return (by_scalar,)

        def inverse_root(sums_of_squares):
            shifted = per_token_tile.tile([P, 1], F32)
            if len(sums_of_squares) == 2:
                nc.gpsimd.tensor_scalar(
                    out=shifted[:], in0=sums_of_squares[0][:], scalar1=sums_of_squares[1][:], scalar2=EPS, op0=ALU.add, op1=ALU.add
                )
            else:
                nc.gpsimd.tensor_scalar(
                    out=shifted[:], in0=sums_of_squares[0][:], scalar1=1.0, scalar2=EPS, op0=ALU.mult, op1=ALU.add
                )
            rstd = per_token_tile.tile([P, 1], F32)
            nc.gpsimd.tensor_tensor(out=rstd[:], in0=shifted[:], in1=minus_half[:], op=ALU.pow)
            return rstd

        def normalise(tt, rstd):
            h = per_token_tile.tile([P, D], BF16)
            nc.vector.scalar_tensor_tensor(
                out=h[:], in0=x_sb[tt][:], scalar=rstd[:], in1=gain[:], op0=ALU.mult, op1=ALU.mult
            )
            return h

        h_grouped, h_codes, h_scales = {}, {}, {}
        w_grouped, w_codes, w_scales = {}, {}, {}

        def flip_and_group(rows, grouped, slot):
            words = rows[:].bitcast(F32)
            bank = flipped.tile([P, WORDS // P, P], F32, tag="bank")
            for gu in range(WORDS // P):
                nc.tensor.transpose(bank[:, gu, :], words[:, gu * P : (gu + 1) * P], ident[:])
            view = grouped[:].bitcast(F32).rearrange("p (g c u) -> p g c u", g=PASSES, u=2)
            nc.scalar.copy(
                out=view[:, :, slot * P : (slot + 1) * P, :], in_=bank[:].rearrange("p (g u) c -> p g c u", g=PASSES)
            )

        def group_w(n, rows=range(ROW_TILES)):
            if n not in w_grouped:
                w_grouped[n] = per_chunk.tile([P, PASSES * CHUNK * PACK], BF16, align_bytes=64, name="w_group")
            for r in rows:
                flip_and_group(w_sb[n, r], w_grouped[n], r)

        def quantise_w(n):
            wc = per_chunk.tile([P, PASSES * CHUNK], U32, align_bytes=64)
            ws = per_chunk.tile([P, PASSES * CHUNK], U8, align_bytes=64)
            parts = PASSES if n == 0 else 1
            words = PASSES * CHUNK // parts
            for part_of in range(parts):
                nc.vector.quantize_mx(
                    out=wc[:, part_of * words : (part_of + 1) * words].bitcast(FP8X4),
                    scales=ws[:, part_of * words : (part_of + 1) * words],
                    in_=w_grouped[n][:, part_of * words * PACK : (part_of + 1) * words * PACK],
                )
            w_codes[n], w_scales[n] = wc, ws

        def group_h(tt, h):
            h_grouped[tt] = per_token_tile.tile([P, PASSES * P * PACK], BF16, align_bytes=64, name="h_group")
            flip_and_group(h, h_grouped[tt], 0)

        def quantise_h(tt):
            hc = per_token_tile.tile([P, PASSES * P], U32, align_bytes=64)
            hs = per_token_tile.tile([P, PASSES * P], U8, align_bytes=64)
            nc.vector.quantize_mx(out=hc[:].bitcast(FP8X4), scales=hs[:], in_=h_grouped[tt][:])
            h_codes[tt], h_scales[tt] = hc, hs

        pairwise = consts.tile([P, TILES_PER_BATCH, 2, DH], F32)
        straight = consts.tile([P, TILES_PER_BATCH, 2, DH], F32)
        across = consts.tile([P, 2, S], F32)

        by_pair = "p j (i r) -> p j i r"

        def sines(out, kind, scale=TWO_PI):
            nc.scalar.activation(out=out, in_=kind, func=ACT.Sin, scale=scale)

        def fill_pairwise():
            first, second = (pairwise[:, :, e].rearrange(by_pair, r=2) for e in range(2))
            sines(first, part[:].rearrange("p r j i -> p j i r"))
            sines(second[:, :, :, 0], part[:, SIN], scale=-TWO_PI)
            sines(second[:, :, :, 1], part[:, COS])

        def fill_straight():
            same, other = (straight[:, :, which].rearrange(by_pair, r=2) for which in range(2))
            shape = [P, TILES_PER_BATCH, PAIRS, 2]
            sines(same, part[:, COS].unsqueeze(3).to_broadcast(shape))
            sines(other[:, :, :, 0], part[:, SIN])
            sines(other[:, :, :, 1], part[:, SIN], scale=-TWO_PI)

        def turn_tables():
            bank = flipped.tile([P, 2, TILES_PER_BATCH, P], F32, tag="bank")
            for which in range(2):
                for j in range(TILES_PER_BATCH):
                    nc.tensor.transpose(bank[:, which, j, :], straight[:, j, which, :], ident[:])
            nc.scalar.copy(out=across[:], in_=bank[:].rearrange("p w j t -> p w (j t)"))

        def in_feature_form(n, tt):
            return tt < 2 and 0 < n < CHUNKS - 1 or (n, tt) == (CHUNKS - 1, 2)

        sums_of, products_of, turned_of = {}, {}, {}

        def multiply(n, tt):
            acc = sums.tile([P, CHUNK], F32)
            if in_feature_form(n, tt):
                for head in range(HEADS):
                    for g in range(PASSES):
                        stationary = slice(g * CHUNK + head * P, g * CHUNK + (head + 1) * P)
                        moving = slice(g * P, (g + 1) * P)
                        nc.tensor.matmul_mx(
                            out=acc[:, head * P : (head + 1) * P],
                            lhsT=w_codes[n][:, stationary].bitcast(FP8X4),
                            lhsT_scale=w_scales[n][:, stationary],
                            rhs=h_codes[tt][:, moving].bitcast(FP8X4),
                            rhs_scale=h_scales[tt][:, moving],
                            start=(g == 0),
                            stop=(g == PASSES - 1),
                        )
            else:
                for g in range(PASSES):
                    stationary = slice(g * P, (g + 1) * P)
                    moving = slice(g * CHUNK, (g + 1) * CHUNK)
                    nc.tensor.matmul_mx(
                        out=acc[:],
                        lhsT=h_codes[tt][:, stationary].bitcast(FP8X4),
                        lhsT_scale=h_scales[tt][:, stationary],
                        rhs=w_codes[n][:, moving].bitcast(FP8X4),
                        rhs_scale=w_scales[n][:, moving],
                        start=(g == 0),
                        stop=(g == PASSES - 1),
                    )
            sums_of[n, tt] = acc

        def form_products(n, tt):
            acc = sums_of.pop((n, tt))
            j = tt % TILES_PER_BATCH
            if in_feature_form(n, tt):
                shape = [P, 2, HEADS, P]
                products = rotating.tile(shape, F32)
                nc.vector.tensor_tensor(
                    out=products[:],
                    in0=acc[:].rearrange("p (h t) -> p h t", t=P).unsqueeze(1).to_broadcast(shape),
                    in1=across[:, :, j * P : (j + 1) * P].unsqueeze(2).to_broadcast(shape),
                    op=ALU.mult,
                )
            else:
                shape = [P, 2, HEADS, PAIRS, 2]
                products = rotating.tile(shape, F32)
                nc.vector.tensor_tensor(
                    out=products[:],
                    in0=acc[:].rearrange("p (h i e) -> p e h i", i=PAIRS, e=2).unsqueeze(4).to_broadcast(shape),
                    in1=pairwise[:, j].rearrange("p e (i r) -> p e i r", r=2).unsqueeze(2).to_broadcast(shape),
                    op=ALU.mult,
                )
            products_of[n, tt] = products

        def add_products(n, tt, adder=nc.gpsimd):
            products = products_of.pop((n, tt))
            b, j = divmod(tt, TILES_PER_BATCH)
            if j == 0:
                turned_of[n, b] = rotating.tile([P, HEADS, TILES_PER_BATCH, DH], F32, name="turned")
            turned = turned_of[n, b]
            if in_feature_form(n, tt):
                bank = back.tile([P, HEADS, DH], F32, tag="bank")
                for head in range(HEADS):
                    for which, order in enumerate((ident, swap)):
                        nc.tensor.matmul(
                            out=bank[:, head, :], lhsT=products[:, which, head, :], rhs=order[:],
                            start=(which == 0), stop=(which == 1), is_transpose=True,
                        )
                nc.scalar.copy(out=turned[:, :, j, :], in_=bank[:])
            else:
                adder.tensor_tensor(
                    out=turned[:, :, j, :],
                    in0=products[:, 0].rearrange("p h i r -> p h (i r)"),
                    in1=products[:, 1].rearrange("p h i r -> p h (i r)"),
                    op=ALU.add,
                )
            matrix, c = divmod(n, CHUNKS_PER_WEIGHT)
            view = (out_0, out_1)[matrix][b, c * HEADS : (c + 1) * HEADS].rearrange("h (p j) d -> p h j d", j=TILES_PER_BATCH)
            if n + 1 == CHUNKS and b + 1 == B:
                nc.sync.dma_start(out=view[:, :, j, :], in_=turned[:, :, j, :])
            elif j + 1 == TILES_PER_BATCH:
                nc.sync.dma_start(out=view, in_=turned[:])

        squares_0 = mean_square(0)
        squares_1 = mean_square(1)
        reduce_angles()
        rstd_0 = inverse_root(squares_0)
        rstd_1 = inverse_root(squares_1)
        rstd_2 = inverse_root(mean_square_on_scalar(2))
        rstd_3 = inverse_root(mean_square_on_scalar(3))
        h0 = normalise(0, rstd_0)
        h1 = normalise(1, rstd_1)
        h2 = normalise(2, rstd_2)
        h3 = normalise(3, rstd_3)
        group_w(0, (0, 1))
        group_h(0, h0)
        group_w(0, (2,))
        group_h(1, h1)
        group_w(0, (3,))
        quantise_h(0)
        quantise_h(1)
        group_h(2, h2)
        quantise_w(0)
        group_h(3, h3)
        fill_pairwise()
        group_w(1, (0,))
        multiply(0, 0)
        quantise_h(2)
        multiply(0, 1)
        quantise_h(3)
        group_w(1, (1, 2, 3))
        fill_straight()
        order = [(n, tt) for n in range(CHUNKS) for tt in range(TOKEN_TILES)]
        for k, (n, tt) in enumerate(order):
            form_products(n, tt)
            vector_adds = (n, tt) == order[-1]
            if vector_adds:
                add_products(n, tt, nc.vector)
            if tt == (2 if n == 0 else 1) and n + 1 < CHUNKS:
                quantise_w(n + 1)
            if k + 2 < len(order):
                multiply(*order[k + 2])
            if not vector_adds:
                add_products(n, tt)
            if k == 1:
                turn_tables()
            if n + 2 < CHUNKS:
                group_w(n + 2, (tt,))
